import numpy as np
import ml_dtypes


def mxq(x, axis, fmt="e4m3"):
    dtype, down = {"e4m3": (ml_dtypes.float8_e4m3fn, 7), "e5m2": (ml_dtypes.float8_e5m2, 14)}[fmt]
    v = np.moveaxis(np.asarray(x, np.float32).astype(ml_dtypes.bfloat16).astype(np.float64), axis, -1)
    blocks = v.reshape(v.shape[:-1] + (-1, 32))
    amax = np.abs(blocks).max(-1, keepdims=True)
    byte = np.maximum(np.where(amax > 0, np.frexp(amax)[1] - 1 + 127, 0) - down, 1)
    scale = np.exp2(byte - 127.0)
    codes = (blocks / scale).astype(np.float32).astype(dtype).astype(np.float64)
    return np.moveaxis((codes * scale).reshape(v.shape), -1, axis)


WIDE = False


def mx_kscale(k):
    if not WIDE:
        return np.ones(k)
    levels = np.array([10, -10, 5, -5, 0])
    if k % 512:
        return np.exp2(np.random.permutation(np.resize(levels, k // 32))).repeat(32)
    a = np.empty((k // 512, 16))
    for p in range(k // 512):
        a[p, :8] = np.random.permutation(np.resize(levels, 8))
        for g in range(8):
            far = levels[np.abs(levels - a[p, g]) >= 10]
            a[p, g + 8] = far[np.random.randint(len(far))]
    return np.exp2(a.ravel()).repeat(32)


BF16 = ml_dtypes.bfloat16


def bf(x):
    return np.asarray(x, np.float32).astype(BF16)


def f64(x):
    return np.asarray(x).astype(np.float64)


E2M1 = np.array([0.0, 0.5, 1.0, 1.5, 2.0, 3.0, 4.0, 6.0, -0.0, -0.5, -1.0, -1.5, -2.0, -3.0, -4.0, -6.0])


def pack_weight(w, fmt):
    k, n = w.shape
    w = f64(bf(w)).reshape(k // 32, 32, n)
    amax = np.abs(w).max(1)
    if fmt == "e4m3":
        byte = np.frexp(amax)[1] - 1 + 127 - 7
    else:
        mant, ex = np.frexp(amax / 6.0)
        byte = np.where(mant > 0.5, ex, ex - 1) + 127
    byte = np.clip(np.where(amax > 0, byte, 1), 1, 254)
    scaled = (w * np.exp2(127.0 - byte)[:, None, :]).reshape(k, n).astype(np.float32)
    by_word = np.ascontiguousarray(scaled.reshape(k // 512, 128, 4, n).transpose(0, 1, 3, 2))
    if fmt == "e4m3":
        words = by_word.astype(ml_dtypes.float8_e4m3fn).view(np.uint8)
    else:
        c = by_word.astype(ml_dtypes.float4_e2m1fn).view(np.uint8) & 0xF
        words = c[..., 0::2] | (c[..., 1::2] << 4)
    return np.ascontiguousarray(words), np.ascontiguousarray(byte.astype(np.uint8).reshape(k // 512, 16, n))


def unpack_weight(words, scales, fmt):
    g, p, n, _ = words.shape
    if fmt == "e4m3":
        vals = np.ascontiguousarray(words).view(ml_dtypes.float8_e4m3fn).astype(np.float64)
    else:
        nib = np.empty((g, p, n, 4), np.uint8)
        nib[..., 0::2] = words & 0xF
        nib[..., 1::2] = words >> 4
        vals = E2M1[nib]
    vals = vals * np.repeat(np.exp2(scales.astype(np.float64) - 127.0), 8, axis=1)[..., None]
    return vals.transpose(0, 1, 3, 2).reshape(g * 512, n)


T, B, F, H, R, O = 1024, 8, 1024, 1024, 512, 128


def draw0():
    s, t = mx_kscale(R), mx_kscale(H)
    z2 = bf(np.random.standard_normal((T, B, R)) * s)
    sw1_words, sw1_scales = pack_weight(np.random.standard_normal((R, H)) / np.sqrt(R) / s[:, None] * t, "e4m3")
    return {"z2": z2,
            "sw1_words": sw1_words,
            "sw1_scales": sw1_scales,
            "b2": bf(np.random.standard_normal((B, H)) * t),
            "w3": bf(np.random.standard_normal((B, H, O)) / np.sqrt(H) / t[:, None]),
            "b3": bf(np.random.standard_normal((B, O)))}


def core(z2, sw1_words, sw1_scales, b2, w3, b3):
    u = (mxq(f64(z2), 2, "e4m3").reshape(T * B, R) @ unpack_weight(sw1_words, sw1_scales, "e4m3")).reshape(T, B, H)
    h = np.maximum(u + f64(b2)[None, :, :], 0.0)
    out = (mxq(h, 2, "e4m3").transpose(1, 0, 2) @ mxq(f64(w3), 1, "e4m3")) + f64(b3)[:, None, :]
    return out.transpose(1, 0, 2)


def e4m3fn_bytes(y):
    return np.clip(np.asarray(y, np.float64), -448.0, 448.0).astype(np.float32).astype(ml_dtypes.float8_e4m3fn).view(np.uint8)


def e4m3fn_values(b):
    return np.asarray(b, np.uint8).view(ml_dtypes.float8_e4m3fn).astype(np.float64)


def setup_inputs():
    d = draw0()
    x0 = np.asarray(d['z2']).astype(np.float64)
    s = (np.max(np.abs(x0), axis=(0, 1), keepdims=True) / 448.0).astype(np.float32)
    out = {}
    for k, v in d.items():
        if k == 'z2':
            out['z2_bytes'] = e4m3fn_bytes(x0 / s.astype(np.float64))
            out['z2_scale'] = s
        else:
            out[k] = v
    return out


def reference(z2_bytes, z2_scale, sw1_words, sw1_scales, b2, w3, b3):
    return core(e4m3fn_values(z2_bytes) * z2_scale.astype(np.float64), sw1_words, sw1_scales, b2, w3, b3)

@@ -1,0 +1,328 @@
+from contextlib import ExitStack
+
+import concourse.mybir as mybir
+from concourse.masks import make_identity
+
+T, B, R, H, O = 1024, 8, 512, 1024, 128
+FLOPS = 2 * T * B * (R * H + H * O)
+
+F32 = mybir.dt.float32
+BF16 = mybir.dt.bfloat16
+U32 = mybir.dt.uint32
+I32 = mybir.dt.int32
+U8 = mybir.dt.uint8
+FP8 = mybir.dt.float8_e4m3fn
+FP8X4 = mybir.dt.float8_e4m3fn_x4
+ALU = mybir.AluOpType
+ACT = mybir.ActivationFunctionType
+
+P = 128
+PACK = 4
+G = H // 512
+ROWS = 512
+SUB = ROWS // P
+HALVES = T // ROWS
+STEPS = B * HALVES
+NT = 192
+
+
+def tile_mlpmodelpredictor_pb_t_w8_kernel(
+    tc, z2_bytes, z2_scale, sw1_words, sw1_scales, b2, w3, b3, out
+):
+    nc = tc.nc
+    with ExitStack() as ctx:
+        keep = ctx.enter_context(tc.tile_pool(name="keep", bufs=1))
+        loads = ctx.enter_context(tc.tile_pool(name="loads", bufs=1))
+        work = ctx.enter_context(tc.tile_pool(name="work", bufs=2))
+        psum = ctx.enter_context(tc.psum_pool(name="psum", bufs=1))
+        ctx.enter_context(tc.manual_schedule())
+
+        warm = keep.tile([P, 1], F32, name="warm")
+        ident_f = keep.tile([P, P], F32, name="ident_f")
+        ident_b = keep.tile([P, P], BF16, name="ident_b")
+        kscale = keep.tile([P, SUB, R], F32, name="kscale")
+        w1_raw = keep.tile([P, H], I32, name="w1_raw", align_bytes=64)
+        w1_codes = keep.tile([P, G, PACK, P], I32, name="w1_codes", align_bytes=64)
+        w1s_raw = keep.tile([P, H], U8, name="w1s_raw", align_bytes=64)
+        w1_scales = keep.tile([P, G, PACK, P], U8, name="w1_scales", align_bytes=64)
+        b2_cols = keep.tile([P, B * G, PACK], BF16, name="b2_cols")
+        b3_rows = keep.tile([P, B, O], BF16, name="b3_rows")
+
+        zbytes = []
+        w3_raw = []
+        for b in range(B):
+            w3_tile = loads.tile([P, G, PACK, O], BF16, name="w3_tile", bufs=B)
+            w3_raw.append(w3_tile)
+            for hf in range(HALVES):
+                zb = loads.tile([P, SUB, R], U8, name="zb", bufs=STEPS, align_bytes=64)
+                zbytes.append(zb)
+
+        def load_z(s):
+            b, hf = divmod(s, HALVES)
+            nc.sync.dma_start(
+                out=zbytes[s][:],
+                in_=z2_bytes[hf * ROWS : (hf + 1) * ROWS, b, :].rearrange("(i p) k -> p i k", p=P),
+            )
+
+        def load_w3(b):
+            nc.sync.dma_start(
+                out=w3_raw[b][:], in_=w3[b].rearrange("(g p j) o -> p g j o", p=P, j=PACK)
+            )
+
+        nc.vector.memset(warm[:], 0.0)
+        nc.vector.memset(w1s_raw[:].bitcast(I32), 0)
+        nc.scalar.dma_start(
+            out=kscale[:, 0, :], in_=z2_scale.rearrange("a c k -> (a c k)").partition_broadcast(P)
+        )
+        nc.scalar.activation(out=warm[:], in_=warm[:], func=ACT.Relu)
+        nc.sync.dma_start(
+            out=w1_raw[:], in_=sw1_words[0].rearrange("p n t -> p (n t)").bitcast(I32)
+        )
+        load_z(0)
+        for q in range(4):
+            nc.sync.dma_start(
+                out=w1s_raw[32 * q : 32 * q + 4, :].bitcast(I32),
+                in_=sw1_scales[0, 4 * q : 4 * q + 4, :].bitcast(I32),
+            )
+        nc.gpsimd.dma_start(
+            out=b2_cols[:],
+            in_=b2.rearrange("b n -> (b n)").rearrange("(c p t) -> p c t", p=P, t=PACK),
+        )
+        make_identity(nc, ident_f[:])
+        make_identity(nc, ident_b[:])
+        load_w3(0)
+        load_z(1)
+        load_z(2)
+        load_z(3)
+        nc.gpsimd.dma_start(
+            out=b3_rows[:].rearrange("p b o -> p (b o)"),
+            in_=b3.rearrange("b o -> (b o)").partition_broadcast(P),
+        )
+        for b in range(1, B):
+            load_w3(b)
+            for s in range(2 * b + 2, min(2 * b + 4, STEPS)):
+                load_z(s)
+
+        zs, zi, zt, zc, zsc = {}, {}, {}, {}, {}
+        hp, hi, hc, hsc, acc1 = {}, {}, {}, {}, {}
+        mixed, acc2, w3i, w3c, w3s = {}, {}, {}, {}, {}
+
+        def scale_z(s, first, count, n):
+            if first == 0:
+                t = work.tile([P, SUB, R], BF16, name="zscaled", bufs=3)
+                zs[s] = t
+            t = zs[s]
+            for i in range(first, first + count, n):
+                rows = slice(i, i + n)
+                nc.vector.tensor_tensor(
+                    out=t[:, rows, :].rearrange("p i k -> p (i k)"),
+                    in0=zbytes[s][:, rows, :].rearrange("p i k -> p (i k)").bitcast(FP8),
+                    in1=kscale[:, 0:n, :].rearrange("p i k -> p (i k)"),
+                    op=ALU.mult,
+                )
+
+        def transpose_z(s):
+            words = zs[s][:].rearrange("p i k -> p (i k)").bitcast(F32)
+            zt[s] = []
+            for half in range(2):
+                bank = psum.tile([P, 2, 2, P], F32, name="zbank", bufs=2)
+                zt[s].append(bank)
+                for i in range(2):
+                    base = 256 * (2 * half + i)
+                    for u in range(2):
+                        nc.tensor.transpose(
+                            bank[:, i, u, :], words[:, base + u : base + 256 : 2], ident_f[:]
+                        )
+
+        def copy_z(s):
+            t = work.tile([P, ROWS, PACK], BF16, name="zinter", bufs=2, align_bytes=64)
+            zi[s] = t
+            words = t[:].rearrange("p n j -> p (n j)").bitcast(F32)
+            for half in range(2):
+                nc.scalar.copy(
+                    out=words[:, 512 * half : 512 * (half + 1)].rearrange(
+                        "p (i r u) -> p i r u", i=2, u=2
+                    ),
+                    in_=zt[s][half][:].rearrange("p i u r -> p i r u"),
+                )
+
+        def quantize_z(s, cols):
+            if cols.start == 0:
+                c = work.tile([P, ROWS], U32, name="zcodes", bufs=2, align_bytes=64)
+                e = work.tile([P, ROWS], U8, name="zexp", bufs=2, align_bytes=64)
+                zc[s], zsc[s] = c, e
+            nc.vector.quantize_mx(
+                out=zc[s][:, cols].bitcast(FP8X4),
+                scales=zsc[s][:, cols],
+                in_=zi[s][:, cols, :].rearrange("p n j -> p (n j)"),
+            )
+
+        def hidden(s, g, cols):
+            for t in range(PACK):
+                if cols.start == 0:
+                    bank = psum.tile([P, ROWS], F32, name="hbank", bufs=4)
+                    acc1[s, g, t] = bank
+                nc.tensor.matmul_mx(
+                    out=acc1[s, g, t][:, cols],
+                    lhsT=w1_codes[:, g, t, :].bitcast(FP8X4),
+                    lhsT_scale=w1_scales[:, g, t, :],
+                    rhs=zc[s][:, cols].bitcast(FP8X4),
+                    rhs_scale=zsc[s][:, cols],
+                    start=True,
+                    stop=True,
+                )
+
+        def relu(s, g, cols):
+            if g == 0 and cols.start == 0:
+                planar = work.tile([P, G, PACK, ROWS], BF16, name="hplanar", bufs=3)
+                inter = work.tile([P, G, ROWS, PACK], BF16, name="hinter", bufs=3, align_bytes=64)
+                hp[s], hi[s] = planar, inter
+            b = s // HALVES
+            for t in range(PACK):
+                nc.scalar.activation(
+                    out=hp[s][:, g, t, cols],
+                    in_=acc1[s, g, t][:, cols],
+                    func=ACT.Relu,
+                    bias=b2_cols[:, b * G + g, t : t + 1],
+                )
+
+        def interleave_vector(s, g):
+            nc.vector.tensor_copy(
+                out=hi[s][:, g, NT:, :].rearrange("p (c i) t -> p c t i", i=4),
+                in_=hp[s][:, g, :, NT:].rearrange("p t (c i) -> p c t i", i=4),
+            )
+
+        def interleave_tensor(s, g):
+            bank = psum.tile([P, NT, PACK], BF16, name="ibank", bufs=1)
+            mixed[s, g] = bank
+            for n in range(0, NT, 96):
+                nc.tensor.matmul(
+                    bank[:, n : n + 96, :],
+                    lhsT=ident_b[:],
+                    rhs=hp[s][:, g, :, n : n + 96].rearrange("p t n -> p n t"),
+                    start=True,
+                    stop=True,
+                )
+
+        def copy_h(s, g):
+            nc.scalar.copy(out=hi[s][:, g, 0:NT, :], in_=mixed[s, g][:])
+
+        def quantize_h(s):
+            c = work.tile([P, G, ROWS], U32, name="hcodes", bufs=2, align_bytes=64)
+            e = work.tile([P, G, ROWS], U8, name="hexp", bufs=2, align_bytes=64)
+            hc[s], hsc[s] = c, e
+            for g in range(G):
+                nc.vector.quantize_mx(
+                    out=c[:, g, :].bitcast(FP8X4),
+                    scales=e[:, g, :],
+                    in_=hi[s][:, g, :, :].rearrange("p n j -> p (n j)"),
+                )
+
+        def interleave_w3(b):
+            t = work.tile([P, G, O, PACK], BF16, name="w3inter", bufs=2, align_bytes=64)
+            w3i[b] = t
+            for g in range(G):
+                nc.vector.tensor_copy(
+                    out=t[:, g, :, :].rearrange("p (c i) t -> p c t i", i=4),
+                    in_=w3_raw[b][:, g, :, :].rearrange("p t (c i) -> p c t i", i=4),
+                )
+
+        def quantize_w3(b):
+            c = work.tile([P, G, O], U32, name="w3codes", bufs=B, align_bytes=64)
+            e = work.tile([P, G, O], U8, name="w3exp", bufs=B, align_bytes=64)
+            w3c[b], w3s[b] = c, e
+            nc.vector.quantize_mx(
+                out=c[:].rearrange("p g o -> p (g o)").bitcast(FP8X4),
+                scales=e[:].rearrange("p g o -> p (g o)"),
+                in_=w3i[b][:].rearrange("p g o j -> p (g o j)"),
+            )
+
+        def output(s):
+            b = s // HALVES
+            bank = psum.tile([P, SUB, O], F32, name="obank", bufs=1)
+            acc2[s] = bank
+            for i in range(SUB):
+                rows = slice(i * P, (i + 1) * P)
+                for g in range(G):
+                    nc.tensor.matmul_mx(
+                        out=bank[:, i, :],
+                        lhsT=hc[s][:, g, rows].bitcast(FP8X4),
+                        lhsT_scale=hsc[s][:, g, rows],
+                        rhs=w3c[b][:, g, :].bitcast(FP8X4),
+                        rhs_scale=w3s[b][:, g, :],
+                        start=(g == 0),
+                        stop=(g == G - 1),
+                    )
+
+        def store(s):
+            b, hf = divmod(s, HALVES)
+            t = work.tile([P, SUB, O], F32, name="result", bufs=3)
+            nc.vector.tensor_tensor(
+                out=t[:],
+                in0=acc2[s][:],
+                in1=b3_rows[:, b, :].unsqueeze(1).to_broadcast([P, SUB, O]),
+                op=ALU.add,
+            )
+            nc.sync.dma_start(
+                out=out[hf * ROWS : (hf + 1) * ROWS, b, :].rearrange("(i p) o -> p i o", p=P),
+                in_=t[:],
+            )
+
+        nc.vector.tensor_copy(
+            out=w1_codes[:], in_=w1_raw[:].rearrange("p (g m t) -> p g t m", g=G, t=PACK)
+        )
+        nc.vector.tensor_copy(
+            out=w1_scales[:], in_=w1s_raw[:].rearrange("p (g m t) -> p g t m", g=G, t=PACK)
+        )
+        whole, left, right = slice(0, ROWS), slice(0, ROWS // 2), slice(ROWS // 2, ROWS)
+        scale_z(0, 0, SUB, 1)
+        transpose_z(0)
+        copy_z(0)
+        for i in range(1, SUB):
+            nc.scalar.copy(out=kscale[:, i, :], in_=kscale[:, 0, :])
+        quantize_z(0, left)
+        scale_z(1, 0, 2, 1)
+        quantize_z(0, right)
+        scale_z(1, 2, 2, 1)
+        interleave_w3(0)
+
+        for s in range(STEPS + 2):
+            parts = [left, right] if s == 0 else [whole]
+            if s < STEPS:
+                for cols in parts:
+                    hidden(s, 0, cols)
+                    if s == 0:
+                        relu(s, 0, cols)
+            if 1 <= s <= STEPS:
+                interleave_vector(s - 1, 1)
+            if s + 1 < STEPS:
+                transpose_z(s + 1)
+            if 1 <= s < STEPS:
+                relu(s, 0, whole)
+            if s + 2 < STEPS:
+                scale_z(s + 2, 0, SUB, SUB)
+            if s + 1 < STEPS:
+                copy_z(s + 1)
+            if 1 <= s <= STEPS:
+                interleave_tensor(s - 1, 1)
+                copy_h(s - 1, 1)
+            if s >= 2:
+                output(s - 2)
+                store(s - 2)
+            if s < STEPS:
+                interleave_vector(s, 0)
+                hidden(s, 1, whole)
+                relu(s, 1, whole)
+                interleave_tensor(s, 0)
+            if s + 1 < STEPS:
+                quantize_z(s + 1, whole)
+            if s < STEPS:
+                copy_h(s, 0)
+            if 1 <= s <= STEPS:
+                quantize_h(s - 1)
+            if s < STEPS:
+                b, hf = divmod(s, HALVES)
+                if hf == 0:
+                    quantize_w3(b)
+                elif b + 1 < B:
+                    interleave_w3(b + 1)

@@ -40,7 +40,7 @@ def tile_mlpmodelpredictor_pb_t_w8_kernel(
         warm = keep.tile([P, 1], F32, name="warm")
         ident_f = keep.tile([P, P], F32, name="ident_f")
         ident_b = keep.tile([P, P], BF16, name="ident_b")
-        kscale = keep.tile([P, SUB, R], F32, name="kscale")
+        kscale = keep.tile([P, PACK], F32, name="kscale")
         w1_raw = keep.tile([P, H], I32, name="w1_raw", align_bytes=64)
         w1_codes = keep.tile([P, G, PACK, P], I32, name="w1_codes", align_bytes=64)
         w1s_raw = keep.tile([P, H], U8, name="w1s_raw", align_bytes=64)
@@ -72,13 +72,14 @@ def tile_mlpmodelpredictor_pb_t_w8_kernel(
         nc.vector.memset(warm[:], 0.0)
         nc.vector.memset(w1s_raw[:].bitcast(I32), 0)
         nc.scalar.dma_start(
-            out=kscale[:, 0, :], in_=z2_scale.rearrange("a c k -> (a c k)").partition_broadcast(P)
+            out=kscale[:], in_=z2_scale.rearrange("a c (p t) -> p (a c t)", t=PACK)
         )
         nc.scalar.activation(out=warm[:], in_=warm[:], func=ACT.Relu)
+        load_z(0)
         nc.sync.dma_start(
             out=w1_raw[:], in_=sw1_words[0].rearrange("p n t -> p (n t)").bitcast(I32)
         )
-        load_z(0)
+        load_z(1)
         for q in range(4):
             nc.sync.dma_start(
                 out=w1s_raw[32 * q : 32 * q + 4, :].bitcast(I32),
@@ -90,9 +91,8 @@ def tile_mlpmodelpredictor_pb_t_w8_kernel(
         )
         make_identity(nc, ident_f[:])
         make_identity(nc, ident_b[:])
-        load_w3(0)
-        load_z(1)
         load_z(2)
+        load_w3(0)
         load_z(3)
         nc.gpsimd.dma_start(
             out=b3_rows[:].rearrange("p b o -> p (b o)"),
@@ -107,18 +107,13 @@ def tile_mlpmodelpredictor_pb_t_w8_kernel(
         hp, hi, hc, hsc, acc1 = {}, {}, {}, {}, {}
         mixed, acc2, w3i, w3c, w3s = {}, {}, {}, {}, {}
 
-        def scale_z(s, first, count, n):
-            if first == 0:
-                t = work.tile([P, SUB, R], BF16, name="zscaled", bufs=3)
-                zs[s] = t
-            t = zs[s]
-            for i in range(first, first + count, n):
-                rows = slice(i, i + n)
-                nc.vector.tensor_tensor(
-                    out=t[:, rows, :].rearrange("p i k -> p (i k)"),
-                    in0=zbytes[s][:, rows, :].rearrange("p i k -> p (i k)").bitcast(FP8),
-                    in1=kscale[:, 0:n, :].rearrange("p i k -> p (i k)"),
-                    op=ALU.mult,
+        def widen_z(s, copy, n):
+            t = work.tile([P, SUB, R], BF16, name="zwide", bufs=4)
+            zs[s] = t
+            for i in range(0, SUB, n):
+                copy(
+                    out=t[:, i : i + n, :].rearrange("p i k -> p (i k)"),
+                    in_=zbytes[s][:, i : i + n, :].rearrange("p i k -> p (i k)").bitcast(FP8),
                 )
 
         def transpose_z(s):
@@ -131,20 +126,26 @@ def tile_mlpmodelpredictor_pb_t_w8_kernel(
                     base = 256 * (2 * half + i)
                     for u in range(2):
                         nc.tensor.transpose(
-                            bank[:, i, u, :], words[:, base + u : base + 256 : 2], ident_f[:]
+                            bank[:, u, i, :], words[:, base + u : base + 256 : 2], ident_f[:]
                         )
 
-        def copy_z(s):
-            t = work.tile([P, ROWS, PACK], BF16, name="zinter", bufs=2, align_bytes=64)
-            zi[s] = t
-            words = t[:].rearrange("p n j -> p (n j)").bitcast(F32)
-            for half in range(2):
-                nc.scalar.copy(
-                    out=words[:, 512 * half : 512 * (half + 1)].rearrange(
-                        "p (i r u) -> p i r u", i=2, u=2
-                    ),
-                    in_=zt[s][half][:].rearrange("p i u r -> p i r u"),
-                )
+        def scale_z(s, half):
+            if half == 0:
+                t = work.tile([P, ROWS, PACK], BF16, name="zinter", bufs=2, align_bytes=64)
+                zi[s] = t
+            n = ROWS // 2
+            nc.vector.tensor_tensor(
+                out=zi[s][:, half * n : (half + 1) * n, :].rearrange("p n (u e) -> p n u e", e=2),
+                in0=zt[s][half][:]
+                .rearrange("p u i r -> p (u i r)")
+                .bitcast(BF16)
+                .rearrange("p (u n e) -> p n u e", u=2, e=2),
+                in1=kscale[:]
+                .rearrange("p (u e) -> p u e", e=2)
+                .unsqueeze(1)
+                .to_broadcast([P, n, 2, 2]),
+                op=ALU.mult,
+            )
 
         def quantize_z(s, cols):
             if cols.start == 0:
@@ -211,12 +212,11 @@ def tile_mlpmodelpredictor_pb_t_w8_kernel(
             c = work.tile([P, G, ROWS], U32, name="hcodes", bufs=2, align_bytes=64)
             e = work.tile([P, G, ROWS], U8, name="hexp", bufs=2, align_bytes=64)
             hc[s], hsc[s] = c, e
-            for g in range(G):
-                nc.vector.quantize_mx(
-                    out=c[:, g, :].bitcast(FP8X4),
-                    scales=e[:, g, :],
-                    in_=hi[s][:, g, :, :].rearrange("p n j -> p (n j)"),
-                )
+            nc.vector.quantize_mx(
+                out=c[:].rearrange("p g n -> p (g n)").bitcast(FP8X4),
+                scales=e[:].rearrange("p g n -> p (g n)"),
+                in_=hi[s][:].rearrange("p g n j -> p (g n j)"),
+            )
 
         def interleave_w3(b):
             t = work.tile([P, G, O, PACK], BF16, name="w3inter", bufs=2, align_bytes=64)
@@ -268,55 +268,52 @@ def tile_mlpmodelpredictor_pb_t_w8_kernel(
                 in_=t[:],
             )
 
+        whole, left, right = slice(0, ROWS), slice(0, ROWS // 2), slice(ROWS // 2, ROWS)
+        widen_z(0, nc.vector.tensor_copy, 1)
+        widen_z(1, nc.scalar.copy, 1)
+        widen_z(2, nc.gpsimd.tensor_copy, 1)
+        transpose_z(0)
         nc.vector.tensor_copy(
             out=w1_codes[:], in_=w1_raw[:].rearrange("p (g m t) -> p g t m", g=G, t=PACK)
         )
+        scale_z(0, 0)
         nc.vector.tensor_copy(
             out=w1_scales[:], in_=w1s_raw[:].rearrange("p (g m t) -> p g t m", g=G, t=PACK)
         )
-        whole, left, right = slice(0, ROWS), slice(0, ROWS // 2), slice(ROWS // 2, ROWS)
-        scale_z(0, 0, SUB, 1)
-        transpose_z(0)
-        copy_z(0)
-        for i in range(1, SUB):
-            nc.scalar.copy(out=kscale[:, i, :], in_=kscale[:, 0, :])
+        scale_z(0, 1)
         quantize_z(0, left)
-        scale_z(1, 0, 2, 1)
-        quantize_z(0, right)
-        scale_z(1, 2, 2, 1)
         interleave_w3(0)
+        quantize_z(0, right)
+        transpose_z(1)
 
         for s in range(STEPS + 2):
             parts = [left, right] if s == 0 else [whole]
             if s < STEPS:
                 for cols in parts:
                     hidden(s, 0, cols)
-                    if s == 0:
-                        relu(s, 0, cols)
+                    relu(s, 0, cols)
+            if s + 3 < STEPS:
+                widen_z(s + 3, nc.gpsimd.tensor_copy, 1)
+            if s + 1 < STEPS:
+                scale_z(s + 1, 0)
+                scale_z(s + 1, 1)
             if 1 <= s <= STEPS:
                 interleave_vector(s - 1, 1)
-            if s + 1 < STEPS:
-                transpose_z(s + 1)
-            if 1 <= s < STEPS:
-                relu(s, 0, whole)
-            if s + 2 < STEPS:
-                scale_z(s + 2, 0, SUB, SUB)
-            if s + 1 < STEPS:
-                copy_z(s + 1)
-            if 1 <= s <= STEPS:
                 interleave_tensor(s - 1, 1)
                 copy_h(s - 1, 1)
             if s >= 2:
                 output(s - 2)
                 store(s - 2)
-            if s < STEPS:
-                interleave_vector(s, 0)
-                hidden(s, 1, whole)
-                relu(s, 1, whole)
-                interleave_tensor(s, 0)
             if s + 1 < STEPS:
                 quantize_z(s + 1, whole)
             if s < STEPS:
+                hidden(s, 1, whole)
+                interleave_vector(s, 0)
+                relu(s, 1, whole)
+            if s + 2 < STEPS:
+                transpose_z(s + 2)
+            if s < STEPS:
+                interleave_tensor(s, 0)
                 copy_h(s, 0)
             if 1 <= s <= STEPS:
                 quantize_h(s - 1)

@@ -23,7 +23,7 @@ ROWS = 512
 SUB = ROWS // P
 HALVES = T // ROWS
 STEPS = B * HALVES
-NT = 192
+NT = 240
 
 
 def tile_mlpmodelpredictor_pb_t_w8_kernel(
@@ -71,11 +71,13 @@ def tile_mlpmodelpredictor_pb_t_w8_kernel(
 
         nc.vector.memset(warm[:], 0.0)
         nc.vector.memset(w1s_raw[:].bitcast(I32), 0)
+        make_identity(nc, ident_f[:])
+        make_identity(nc, ident_b[:])
+        load_z(0)
         nc.scalar.dma_start(
             out=kscale[:], in_=z2_scale.rearrange("a c (p t) -> p (a c t)", t=PACK)
         )
         nc.scalar.activation(out=warm[:], in_=warm[:], func=ACT.Relu)
-        load_z(0)
         nc.sync.dma_start(
             out=w1_raw[:], in_=sw1_words[0].rearrange("p n t -> p (n t)").bitcast(I32)
         )
@@ -85,20 +87,21 @@ def tile_mlpmodelpredictor_pb_t_w8_kernel(
                 out=w1s_raw[32 * q : 32 * q + 4, :].bitcast(I32),
                 in_=sw1_scales[0, 4 * q : 4 * q + 4, :].bitcast(I32),
             )
-        nc.gpsimd.dma_start(
+        nc.sync.dma_start(
             out=b2_cols[:],
             in_=b2.rearrange("b n -> (b n)").rearrange("(c p t) -> p c t", p=P, t=PACK),
         )
-        make_identity(nc, ident_f[:])
-        make_identity(nc, ident_b[:])
-        load_z(2)
         load_w3(0)
+        load_z(2)
         load_z(3)
-        nc.gpsimd.dma_start(
+        load_z(4)
+        load_w3(1)
+        load_z(5)
+        nc.sync.dma_start(
             out=b3_rows[:].rearrange("p b o -> p (b o)"),
             in_=b3.rearrange("b o -> (b o)").partition_broadcast(P),
         )
-        for b in range(1, B):
+        for b in range(2, B):
             load_w3(b)
             for s in range(2 * b + 2, min(2 * b + 4, STEPS)):
                 load_z(s)
@@ -107,19 +110,16 @@ def tile_mlpmodelpredictor_pb_t_w8_kernel(
         hp, hi, hc, hsc, acc1 = {}, {}, {}, {}, {}
         mixed, acc2, w3i, w3c, w3s = {}, {}, {}, {}, {}
 
-        def widen_z(s, copy, n):
-            t = work.tile([P, SUB, R], BF16, name="zwide", bufs=4)
+        def widen_z(s, copies):
+            t = work.tile([P, SUB, R], BF16, name="zwide", bufs=2)
             zs[s] = t
-            for i in range(0, SUB, n):
-                copy(
-                    out=t[:, i : i + n, :].rearrange("p i k -> p (i k)"),
-                    in_=zbytes[s][:, i : i + n, :].rearrange("p i k -> p (i k)").bitcast(FP8),
-                )
+            for i, copy in enumerate(copies):
+                copy(out=t[:, i, :], in_=zbytes[s][:, i, :].bitcast(FP8))
 
-        def transpose_z(s):
+        def transpose_z(s, halves):
             words = zs[s][:].rearrange("p i k -> p (i k)").bitcast(F32)
-            zt[s] = []
-            for half in range(2):
+            zt.setdefault(s, [])
+            for half in halves:
                 bank = psum.tile([P, 2, 2, P], F32, name="zbank", bufs=2)
                 zt[s].append(bank)
                 for i in range(2):
@@ -158,8 +158,8 @@ def tile_mlpmodelpredictor_pb_t_w8_kernel(
                 in_=zi[s][:, cols, :].rearrange("p n j -> p (n j)"),
             )
 
-        def hidden(s, g, cols):
-            for t in range(PACK):
+        def hidden(s, g, cols, slots):
+            for t in slots:
                 if cols.start == 0:
                     bank = psum.tile([P, ROWS], F32, name="hbank", bufs=4)
                     acc1[s, g, t] = bank
@@ -176,7 +176,7 @@ def tile_mlpmodelpredictor_pb_t_w8_kernel(
         def relu(s, g, cols):
             if g == 0 and cols.start == 0:
                 planar = work.tile([P, G, PACK, ROWS], BF16, name="hplanar", bufs=3)
-                inter = work.tile([P, G, ROWS, PACK], BF16, name="hinter", bufs=3, align_bytes=64)
+                inter = work.tile([P, G, ROWS, PACK], BF16, name="hinter", bufs=4, align_bytes=64)
                 hp[s], hi[s] = planar, inter
             b = s // HALVES
             for t in range(PACK):
@@ -187,20 +187,20 @@ def tile_mlpmodelpredictor_pb_t_w8_kernel(
                     bias=b2_cols[:, b * G + g, t : t + 1],
                 )
 
-        def interleave_vector(s, g):
+        def interleave_vector(s):
             nc.vector.tensor_copy(
-                out=hi[s][:, g, NT:, :].rearrange("p (c i) t -> p c t i", i=4),
-                in_=hp[s][:, g, :, NT:].rearrange("p t (c i) -> p c t i", i=4),
+                out=hi[s][:, :, NT:, :].rearrange("p g (c i) t -> p g c t i", i=4),
+                in_=hp[s][:, :, :, NT:].rearrange("p g t (c i) -> p g c t i", i=4),
             )
 
         def interleave_tensor(s, g):
             bank = psum.tile([P, NT, PACK], BF16, name="ibank", bufs=1)
             mixed[s, g] = bank
-            for n in range(0, NT, 96):
+            for n in range(0, NT, NT // 2):
                 nc.tensor.matmul(
-                    bank[:, n : n + 96, :],
+                    bank[:, n : n + NT // 2, :],
                     lhsT=ident_b[:],
-                    rhs=hp[s][:, g, :, n : n + 96].rearrange("p t n -> p n t"),
+                    rhs=hp[s][:, g, :, n : n + NT // 2].rearrange("p t n -> p n t"),
                     start=True,
                     stop=True,
                 )
@@ -218,14 +218,13 @@ def tile_mlpmodelpredictor_pb_t_w8_kernel(
                 in_=hi[s][:].rearrange("p g n j -> p (g n j)"),
             )
 
-        def interleave_w3(b):
+        def interleave_w3(b, copy):
             t = work.tile([P, G, O, PACK], BF16, name="w3inter", bufs=2, align_bytes=64)
             w3i[b] = t
-            for g in range(G):
-                nc.vector.tensor_copy(
-                    out=t[:, g, :, :].rearrange("p (c i) t -> p c t i", i=4),
-                    in_=w3_raw[b][:, g, :, :].rearrange("p t (c i) -> p c t i", i=4),
-                )
+            copy(
+                out=t[:].rearrange("p g (c i) t -> p g c t i", i=4),
+                in_=w3_raw[b][:].rearrange("p g t (c i) -> p g c t i", i=4),
+            )
 
         def quantize_w3(b):
             c = work.tile([P, G, O], U32, name="w3codes", bufs=B, align_bytes=64)
@@ -269,57 +268,63 @@ def tile_mlpmodelpredictor_pb_t_w8_kernel(
             )
 
         whole, left, right = slice(0, ROWS), slice(0, ROWS // 2), slice(ROWS // 2, ROWS)
-        widen_z(0, nc.vector.tensor_copy, 1)
-        widen_z(1, nc.scalar.copy, 1)
-        widen_z(2, nc.gpsimd.tensor_copy, 1)
-        transpose_z(0)
+        on_v, on_s, on_g = nc.vector.tensor_copy, nc.scalar.copy, nc.gpsimd.tensor_copy
+        widen_z(0, [on_v, on_v, on_v, on_s])
+        widen_z(1, [on_s, on_s, on_s, on_s])
+        interleave_w3(0, on_s)
+        transpose_z(0, [0, 1])
+        scale_z(0, 0)
         nc.vector.tensor_copy(
             out=w1_codes[:], in_=w1_raw[:].rearrange("p (g m t) -> p g t m", g=G, t=PACK)
         )
-        scale_z(0, 0)
+        quantize_z(0, left)
         nc.vector.tensor_copy(
             out=w1_scales[:], in_=w1s_raw[:].rearrange("p (g m t) -> p g t m", g=G, t=PACK)
         )
+        transpose_z(1, [0])
+        hidden(0, 0, left, range(PACK))
+        relu(0, 0, left)
         scale_z(0, 1)
-        quantize_z(0, left)
-        interleave_w3(0)
+        transpose_z(1, [1])
+        scale_z(1, 0)
         quantize_z(0, right)
-        transpose_z(1)
+        scale_z(1, 1)
+        hidden(0, 0, right, range(PACK))
+        relu(0, 0, right)
+        widen_z(2, [on_g] * SUB)
+        widen_z(3, [on_g] * SUB)
 
         for s in range(STEPS + 2):
-            parts = [left, right] if s == 0 else [whole]
-            if s < STEPS:
-                for cols in parts:
-                    hidden(s, 0, cols)
-                    relu(s, 0, cols)
-            if s + 3 < STEPS:
-                widen_z(s + 3, nc.gpsimd.tensor_copy, 1)
-            if s + 1 < STEPS:
-                scale_z(s + 1, 0)
-                scale_z(s + 1, 1)
+            if 1 <= s < STEPS:
+                hidden(s, 0, whole, range(PACK))
+                relu(s, 0, whole)
             if 1 <= s <= STEPS:
-                interleave_vector(s - 1, 1)
+                interleave_vector(s - 1)
                 interleave_tensor(s - 1, 1)
                 copy_h(s - 1, 1)
-            if s >= 2:
-                output(s - 2)
-                store(s - 2)
             if s + 1 < STEPS:
                 quantize_z(s + 1, whole)
+            if s >= 2:
+                quantize_h(s - 2)
             if s < STEPS:
-                hidden(s, 1, whole)
-                interleave_vector(s, 0)
-                relu(s, 1, whole)
-            if s + 2 < STEPS:
-                transpose_z(s + 2)
-            if s < STEPS:
-                interleave_tensor(s, 0)
-                copy_h(s, 0)
-            if 1 <= s <= STEPS:
-                quantize_h(s - 1)
-            if s < STEPS:
+                hidden(s, 1, whole, (0, 1))
                 b, hf = divmod(s, HALVES)
                 if hf == 0:
                     quantize_w3(b)
                 elif b + 1 < B:
-                    interleave_w3(b + 1)
+                    interleave_w3(b + 1, on_v)
+            if s + 2 < STEPS:
+                transpose_z(s + 2, [0, 1])
+                scale_z(s + 2, 0)
+                scale_z(s + 2, 1)
+            if s + 4 < STEPS:
+                widen_z(s + 4, [on_g] * SUB)
+            if s < STEPS:
+                hidden(s, 1, whole, (2, 3))
+                relu(s, 1, whole)
+            if s >= 2:
+                output(s - 2)
+                store(s - 2)
+            if s < STEPS:
+                interleave_tensor(s, 0)
+                copy_h(s, 0)

@@ -23,7 +23,7 @@ ROWS = 512
 SUB = ROWS // P
 HALVES = T // ROWS
 STEPS = B * HALVES
-NT = 240
+NT = 256
 
 
 def tile_mlpmodelpredictor_pb_t_w8_kernel(
@@ -41,7 +41,7 @@ def tile_mlpmodelpredictor_pb_t_w8_kernel(
         ident_f = keep.tile([P, P], F32, name="ident_f")
         ident_b = keep.tile([P, P], BF16, name="ident_b")
         kscale = keep.tile([P, PACK], F32, name="kscale")
-        w1_raw = keep.tile([P, H], I32, name="w1_raw", align_bytes=64)
+        w1_raw = keep.tile([P, G, H // G], I32, name="w1_raw", align_bytes=64)
         w1_codes = keep.tile([P, G, PACK, P], I32, name="w1_codes", align_bytes=64)
         w1s_raw = keep.tile([P, H], U8, name="w1s_raw", align_bytes=64)
         w1_scales = keep.tile([P, G, PACK, P], U8, name="w1_scales", align_bytes=64)
@@ -57,12 +57,14 @@ def tile_mlpmodelpredictor_pb_t_w8_kernel(
                 zb = loads.tile([P, SUB, R], U8, name="zb", bufs=STEPS, align_bytes=64)
                 zbytes.append(zb)
 
-        def load_z(s):
+        def load_z(s, n=SUB):
             b, hf = divmod(s, HALVES)
-            nc.sync.dma_start(
-                out=zbytes[s][:],
-                in_=z2_bytes[hf * ROWS : (hf + 1) * ROWS, b, :].rearrange("(i p) k -> p i k", p=P),
-            )
+            for i in range(0, SUB, n):
+                row = hf * ROWS + i * P
+                nc.sync.dma_start(
+                    out=zbytes[s][:, i : i + n, :],
+                    in_=z2_bytes[row : row + n * P, b, :].rearrange("(i p) k -> p i k", p=P),
+                )
 
         def load_w3(b):
             nc.sync.dma_start(
@@ -73,20 +75,21 @@ def tile_mlpmodelpredictor_pb_t_w8_kernel(
         nc.vector.memset(w1s_raw[:].bitcast(I32), 0)
         make_identity(nc, ident_f[:])
         make_identity(nc, ident_b[:])
-        load_z(0)
+        load_z(0, 2)
         nc.scalar.dma_start(
             out=kscale[:], in_=z2_scale.rearrange("a c (p t) -> p (a c t)", t=PACK)
         )
         nc.scalar.activation(out=warm[:], in_=warm[:], func=ACT.Relu)
-        nc.sync.dma_start(
-            out=w1_raw[:], in_=sw1_words[0].rearrange("p n t -> p (n t)").bitcast(I32)
-        )
-        load_z(1)
+        w1_words = sw1_words[0].rearrange("p n t -> p (n t)").bitcast(I32)
+        for g in range(G):
+            cols = slice(g * H // G, (g + 1) * H // G)
+            nc.sync.dma_start(out=w1_raw[:, g, :], in_=w1_words[:, cols])
         for q in range(4):
             nc.sync.dma_start(
                 out=w1s_raw[32 * q : 32 * q + 4, :].bitcast(I32),
                 in_=sw1_scales[0, 4 * q : 4 * q + 4, :].bitcast(I32),
             )
+        load_z(1)
         nc.sync.dma_start(
             out=b2_cols[:],
             in_=b2.rearrange("b n -> (b n)").rearrange("(c p t) -> p c t", p=P, t=PACK),
@@ -110,8 +113,17 @@ def tile_mlpmodelpredictor_pb_t_w8_kernel(
         hp, hi, hc, hsc, acc1 = {}, {}, {}, {}, {}
         mixed, acc2, w3i, w3c, w3s = {}, {}, {}, {}, {}
 
+        def permute_w1(g):
+            nc.vector.tensor_copy(
+                out=w1_codes[:, g], in_=w1_raw[:, g].rearrange("p (m t) -> p t m", t=PACK)
+            )
+            nc.gpsimd.tensor_copy(
+                out=w1_scales[:, g],
+                in_=w1s_raw[:, g * H // G : (g + 1) * H // G].rearrange("p (m t) -> p t m", t=PACK),
+            )
+
         def widen_z(s, copies):
-            t = work.tile([P, SUB, R], BF16, name="zwide", bufs=2)
+            t = work.tile([P, SUB, R], BF16, name="zwide", bufs=4)
             zs[s] = t
             for i, copy in enumerate(copies):
                 copy(out=t[:, i, :], in_=zbytes[s][:, i, :].bitcast(FP8))
@@ -187,10 +199,10 @@ def tile_mlpmodelpredictor_pb_t_w8_kernel(
                     bias=b2_cols[:, b * G + g, t : t + 1],
                 )
 
-        def interleave_vector(s):
+        def interleave_vector(s, passes, cols):
             nc.vector.tensor_copy(
-                out=hi[s][:, :, NT:, :].rearrange("p g (c i) t -> p g c t i", i=4),
-                in_=hp[s][:, :, :, NT:].rearrange("p g t (c i) -> p g c t i", i=4),
+                out=hi[s][:, passes, cols, :].rearrange("p g (c i) t -> p g c t i", i=4),
+                in_=hp[s][:, passes, :, cols].rearrange("p g t (c i) -> p g c t i", i=4),
             )
 
         def interleave_tensor(s, g):
@@ -206,25 +218,45 @@ def tile_mlpmodelpredictor_pb_t_w8_kernel(
                 )
 
         def copy_h(s, g):
-            nc.scalar.copy(out=hi[s][:, g, 0:NT, :], in_=mixed[s, g][:])
+            nc.scalar.copy(
+                out=hi[s][:, g, 0:NT, :].rearrange("p n j -> p (n j)").bitcast(F32),
+                in_=mixed[s, g][:].rearrange("p n j -> p (n j)").bitcast(F32),
+            )
 
-        def quantize_h(s):
+        def quantize_h_part(s, g, cols):
+            nc.vector.quantize_mx(
+                out=hc[s][:, g, cols].bitcast(FP8X4),
+                scales=hsc[s][:, g, cols],
+                in_=hi[s][:, g, cols, :].rearrange("p n j -> p (n j)"),
+            )
+
+        def new_hidden_codes(s):
             c = work.tile([P, G, ROWS], U32, name="hcodes", bufs=2, align_bytes=64)
             e = work.tile([P, G, ROWS], U8, name="hexp", bufs=2, align_bytes=64)
             hc[s], hsc[s] = c, e
+
+        def quantize_h(s):
+            new_hidden_codes(s)
+            c, e = hc[s], hsc[s]
             nc.vector.quantize_mx(
                 out=c[:].rearrange("p g n -> p (g n)").bitcast(FP8X4),
                 scales=e[:].rearrange("p g n -> p (g n)"),
                 in_=hi[s][:].rearrange("p g n j -> p (g n j)"),
             )
 
-        def interleave_w3(b, copy):
+        def interleave_w3(b):
             t = work.tile([P, G, O, PACK], BF16, name="w3inter", bufs=2, align_bytes=64)
             w3i[b] = t
-            copy(
-                out=t[:].rearrange("p g (c i) t -> p g c t i", i=4),
-                in_=w3_raw[b][:].rearrange("p g t (c i) -> p g c t i", i=4),
-            )
+            if b % 2 == 0:
+                nc.scalar.copy(
+                    out=t[:].rearrange("p g (c i) t -> p g c t i", i=4),
+                    in_=w3_raw[b][:].rearrange("p g t (c i) -> p g c t i", i=4),
+                )
+            else:
+                for g in range(G):
+                    nc.gpsimd.tensor_copy(
+                        out=t[:, g], in_=w3_raw[b][:, g].rearrange("p t o -> p o t")
+                    )
 
         def quantize_w3(b):
             c = work.tile([P, G, O], U32, name="w3codes", bufs=B, align_bytes=64)
@@ -236,11 +268,13 @@ def tile_mlpmodelpredictor_pb_t_w8_kernel(
                 in_=w3i[b][:].rearrange("p g o j -> p (g o j)"),
             )
 
-        def output(s):
+        def output(s, tiles):
             b = s // HALVES
-            bank = psum.tile([P, SUB, O], F32, name="obank", bufs=1)
-            acc2[s] = bank
-            for i in range(SUB):
+            if tiles.start == 0:
+                bank = psum.tile([P, SUB, O], F32, name="obank", bufs=1)
+                acc2[s] = bank
+            bank = acc2[s]
+            for i in tiles:
                 rows = slice(i * P, (i + 1) * P)
                 for g in range(G):
                     nc.tensor.matmul_mx(
@@ -253,34 +287,32 @@ def tile_mlpmodelpredictor_pb_t_w8_kernel(
                         stop=(g == G - 1),
                     )
 
-        def store(s):
+        def store(s, tiles):
             b, hf = divmod(s, HALVES)
+            n = len(tiles)
             t = work.tile([P, SUB, O], F32, name="result", bufs=3)
             nc.vector.tensor_tensor(
-                out=t[:],
-                in0=acc2[s][:],
-                in1=b3_rows[:, b, :].unsqueeze(1).to_broadcast([P, SUB, O]),
+                out=t[:, 0:n, :],
+                in0=acc2[s][:, tiles.start : tiles.stop, :],
+                in1=b3_rows[:, b, :].unsqueeze(1).to_broadcast([P, n, O]),
                 op=ALU.add,
             )
+            row = hf * ROWS + tiles.start * P
             nc.sync.dma_start(
-                out=out[hf * ROWS : (hf + 1) * ROWS, b, :].rearrange("(i p) o -> p i o", p=P),
-                in_=t[:],
+                out=out[row : row + n * P, b, :].rearrange("(i p) o -> p i o", p=P),
+                in_=t[:, 0:n, :],
             )
 
         whole, left, right = slice(0, ROWS), slice(0, ROWS // 2), slice(ROWS // 2, ROWS)
+        both, rest = slice(0, G), slice(NT, ROWS)
         on_v, on_s, on_g = nc.vector.tensor_copy, nc.scalar.copy, nc.gpsimd.tensor_copy
-        widen_z(0, [on_v, on_v, on_v, on_s])
+        widen_z(0, [on_v, on_s, on_v, on_s])
         widen_z(1, [on_s, on_s, on_s, on_s])
-        interleave_w3(0, on_s)
+        interleave_w3(0)
         transpose_z(0, [0, 1])
         scale_z(0, 0)
-        nc.vector.tensor_copy(
-            out=w1_codes[:], in_=w1_raw[:].rearrange("p (g m t) -> p g t m", g=G, t=PACK)
-        )
+        permute_w1(0)
         quantize_z(0, left)
-        nc.vector.tensor_copy(
-            out=w1_scales[:], in_=w1s_raw[:].rearrange("p (g m t) -> p g t m", g=G, t=PACK)
-        )
         transpose_z(1, [0])
         hidden(0, 0, left, range(PACK))
         relu(0, 0, left)
@@ -288,43 +320,61 @@ def tile_mlpmodelpredictor_pb_t_w8_kernel(
         transpose_z(1, [1])
         scale_z(1, 0)
         quantize_z(0, right)
+        permute_w1(1)
         scale_z(1, 1)
         hidden(0, 0, right, range(PACK))
         relu(0, 0, right)
         widen_z(2, [on_g] * SUB)
         widen_z(3, [on_g] * SUB)
 
-        for s in range(STEPS + 2):
-            if 1 <= s < STEPS:
+        last = STEPS - 1
+        for s in range(STEPS):
+            if s >= 1:
                 hidden(s, 0, whole, range(PACK))
                 relu(s, 0, whole)
-            if 1 <= s <= STEPS:
-                interleave_vector(s - 1)
+                interleave_vector(s - 1, both, rest)
                 interleave_tensor(s - 1, 1)
                 copy_h(s - 1, 1)
             if s + 1 < STEPS:
                 quantize_z(s + 1, whole)
             if s >= 2:
                 quantize_h(s - 2)
-            if s < STEPS:
-                hidden(s, 1, whole, (0, 1))
-                b, hf = divmod(s, HALVES)
-                if hf == 0:
-                    quantize_w3(b)
-                elif b + 1 < B:
-                    interleave_w3(b + 1, on_v)
+            hidden(s, 1, whole, (0, 1))
+            if s % HALVES == 0:
+                quantize_w3(s // HALVES)
             if s + 2 < STEPS:
                 transpose_z(s + 2, [0, 1])
                 scale_z(s + 2, 0)
                 scale_z(s + 2, 1)
             if s + 4 < STEPS:
                 widen_z(s + 4, [on_g] * SUB)
-            if s < STEPS:
-                hidden(s, 1, whole, (2, 3))
+            if s % HALVES == 0 and s // HALVES + 1 < B:
+                interleave_w3(s // HALVES + 1)
+            hidden(s, 1, whole, (2, 3))
+            if s < last:
                 relu(s, 1, whole)
-            if s >= 2:
-                output(s - 2)
-                store(s - 2)
-            if s < STEPS:
+                if s >= 2:
+                    output(s - 2, range(SUB))
+                    store(s - 2, range(SUB))
                 interleave_tensor(s, 0)
                 copy_h(s, 0)
+
+        relu(last, 1, left)
+        interleave_vector(last, slice(0, 1), rest)
+        output(last - 2, range(SUB))
+        interleave_tensor(last, 0)
+        copy_h(last, 0)
+        relu(last, 1, right)
+        store(last - 2, range(SUB))
+        quantize_h(last - 1)
+        interleave_vector(last, slice(1, 2), left)
+        output(last - 1, range(SUB))
+        new_hidden_codes(last)
+        quantize_h_part(last, 0, whole)
+        interleave_vector(last, slice(1, 2), right)
+        store(last - 1, range(SUB))
+        for cols, tiles in ((left, range(0, 2)), (right, range(2, 4))):
+            quantize_h_part(last, 1, cols)
+            output(last, tiles)
+        for tiles in (range(0, 2), range(2, 4)):
+            store(last, tiles)

@@ -23,7 +23,7 @@ ROWS = 512
 SUB = ROWS // P
 HALVES = T // ROWS
 STEPS = B * HALVES
-NT = 256
+NT = 240
 
 
 def tile_mlpmodelpredictor_pb_t_w8_kernel(
@@ -45,6 +45,7 @@ def tile_mlpmodelpredictor_pb_t_w8_kernel(
         w1_codes = keep.tile([P, G, PACK, P], I32, name="w1_codes", align_bytes=64)
         w1s_raw = keep.tile([P, H], U8, name="w1s_raw", align_bytes=64)
         w1_scales = keep.tile([P, G, PACK, P], U8, name="w1_scales", align_bytes=64)
+        b2_rows = keep.tile([P, H // G], BF16, name="b2_rows")
         b2_cols = keep.tile([P, B * G, PACK], BF16, name="b2_cols")
         b3_rows = keep.tile([P, B, O], BF16, name="b3_rows")
 
@@ -72,12 +73,16 @@ def tile_mlpmodelpredictor_pb_t_w8_kernel(
             )
 
         nc.vector.memset(warm[:], 0.0)
+        nc.vector.memset(b2_rows[:], 0.0)
         nc.vector.memset(w1s_raw[:].bitcast(I32), 0)
         make_identity(nc, ident_f[:])
         make_identity(nc, ident_b[:])
         load_z(0, 2)
         nc.scalar.dma_start(
             out=kscale[:], in_=z2_scale.rearrange("a c (p t) -> p (a c t)", t=PACK)
+        )
+        nc.scalar.dma_start(
+            out=b2_rows[0 : B * G, :], in_=b2.rearrange("b (g n) -> (b g) n", g=G)
         )
         nc.scalar.activation(out=warm[:], in_=warm[:], func=ACT.Relu)
         w1_words = sw1_words[0].rearrange("p n t -> p (n t)").bitcast(I32)
@@ -90,10 +95,6 @@ def tile_mlpmodelpredictor_pb_t_w8_kernel(
                 in_=sw1_scales[0, 4 * q : 4 * q + 4, :].bitcast(I32),
             )
         load_z(1)
-        nc.sync.dma_start(
-            out=b2_cols[:],
-            in_=b2.rearrange("b n -> (b n)").rearrange("(c p t) -> p c t", p=P, t=PACK),
-        )
         load_w3(0)
         load_z(2)
         load_z(3)
@@ -117,13 +118,13 @@ def tile_mlpmodelpredictor_pb_t_w8_kernel(
             nc.vector.tensor_copy(
                 out=w1_codes[:, g], in_=w1_raw[:, g].rearrange("p (m t) -> p t m", t=PACK)
             )
-            nc.gpsimd.tensor_copy(
+            nc.vector.tensor_copy(
                 out=w1_scales[:, g],
                 in_=w1s_raw[:, g * H // G : (g + 1) * H // G].rearrange("p (m t) -> p t m", t=PACK),
             )
 
         def widen_z(s, copies):
-            t = work.tile([P, SUB, R], BF16, name="zwide", bufs=4)
+            t = work.tile([P, SUB, R], BF16, name="zwide", bufs=2)
             zs[s] = t
             for i, copy in enumerate(copies):
                 copy(out=t[:, i, :], in_=zbytes[s][:, i, :].bitcast(FP8))
@@ -218,10 +219,7 @@ def tile_mlpmodelpredictor_pb_t_w8_kernel(
                 )
 
         def copy_h(s, g):
-            nc.scalar.copy(
-                out=hi[s][:, g, 0:NT, :].rearrange("p n j -> p (n j)").bitcast(F32),
-                in_=mixed[s, g][:].rearrange("p n j -> p (n j)").bitcast(F32),
-            )
+            nc.scalar.copy(out=hi[s][:, g, 0:NT, :], in_=mixed[s, g][:])
 
         def quantize_h_part(s, g, cols):
             nc.vector.quantize_mx(
@@ -247,16 +245,11 @@ def tile_mlpmodelpredictor_pb_t_w8_kernel(
         def interleave_w3(b):
             t = work.tile([P, G, O, PACK], BF16, name="w3inter", bufs=2, align_bytes=64)
             w3i[b] = t
-            if b % 2 == 0:
-                nc.scalar.copy(
-                    out=t[:].rearrange("p g (c i) t -> p g c t i", i=4),
-                    in_=w3_raw[b][:].rearrange("p g t (c i) -> p g c t i", i=4),
-                )
-            else:
-                for g in range(G):
-                    nc.gpsimd.tensor_copy(
-                        out=t[:, g], in_=w3_raw[b][:, g].rearrange("p t o -> p o t")
-                    )
+            copy = nc.scalar.copy if b % 2 == 0 else nc.vector.tensor_copy
+            copy(
+                out=t[:].rearrange("p g (c i) t -> p g c t i", i=4),
+                in_=w3_raw[b][:].rearrange("p g t (c i) -> p g c t i", i=4),
+            )
 
         def quantize_w3(b):
             c = work.tile([P, G, O], U32, name="w3codes", bufs=B, align_bytes=64)
@@ -310,6 +303,14 @@ def tile_mlpmodelpredictor_pb_t_w8_kernel(
         widen_z(1, [on_s, on_s, on_s, on_s])
         interleave_w3(0)
         transpose_z(0, [0, 1])
+        bank = psum.tile([P, SUB, O], F32, name="obank", bufs=1)
+        b2_words = b2_rows[:].bitcast(F32)
+        for u in range(2):
+            nc.tensor.transpose(bank[:, u, :], b2_words[:, u::2], ident_f[:])
+        nc.scalar.copy(
+            out=b2_cols[:].rearrange("p c t -> p (c t)").bitcast(F32).rearrange("p (c u) -> p c u", u=2),
+            in_=bank[:, 0:2, 0 : B * G].rearrange("p u c -> p c u"),
+        )
         scale_z(0, 0)
         permute_w1(0)
         quantize_z(0, left)
@@ -348,7 +349,7 @@ def tile_mlpmodelpredictor_pb_t_w8_kernel(
                 scale_z(s + 2, 1)
             if s + 4 < STEPS:
                 widen_z(s + 4, [on_g] * SUB)
-            if s % HALVES == 0 and s // HALVES + 1 < B:
+            if s % HALVES == 1 and s // HALVES + 1 < B:
                 interleave_w3(s // HALVES + 1)
             hidden(s, 1, whole, (2, 3))
             if s < last:

from contextlib import ExitStack

import concourse.mybir as mybir
from concourse.masks import make_identity

T, B, R, H, O = 1024, 8, 512, 1024, 128
FLOPS = 2 * T * B * (R * H + H * O)

F32 = mybir.dt.float32
BF16 = mybir.dt.bfloat16
U32 = mybir.dt.uint32
I32 = mybir.dt.int32
U8 = mybir.dt.uint8
FP8 = mybir.dt.float8_e4m3fn
FP8X4 = mybir.dt.float8_e4m3fn_x4
ALU = mybir.AluOpType
ACT = mybir.ActivationFunctionType

P = 128
PACK = 4
G = H // 512
ROWS = 512
SUB = ROWS // P
HALVES = T // ROWS
STEPS = B * HALVES
NT = 240


def tile_mlpmodelpredictor_pb_t_w8_kernel(
    tc, z2_bytes, z2_scale, sw1_words, sw1_scales, b2, w3, b3, out
):
    nc = tc.nc
    with ExitStack() as ctx:
        keep = ctx.enter_context(tc.tile_pool(name="keep", bufs=1))
        loads = ctx.enter_context(tc.tile_pool(name="loads", bufs=1))
        work = ctx.enter_context(tc.tile_pool(name="work", bufs=2))
        psum = ctx.enter_context(tc.psum_pool(name="psum", bufs=1))
        ctx.enter_context(tc.manual_schedule())

        warm = keep.tile([P, 1], F32, name="warm")
        ident_f = keep.tile([P, P], F32, name="ident_f")
        ident_b = keep.tile([P, P], BF16, name="ident_b")
        kscale = keep.tile([P, PACK], F32, name="kscale")
        w1_raw = keep.tile([P, G, H // G], I32, name="w1_raw", align_bytes=64)
        w1_codes = keep.tile([P, G, PACK, P], I32, name="w1_codes", align_bytes=64)
        w1s_raw = keep.tile([P, H], U8, name="w1s_raw", align_bytes=64)
        w1_scales = keep.tile([P, G, PACK, P], U8, name="w1_scales", align_bytes=64)
        b2_rows = keep.tile([P, H // G], BF16, name="b2_rows")
        b2_cols = keep.tile([P, B * G, PACK], BF16, name="b2_cols")
        b3_rows = keep.tile([P, B, O], BF16, name="b3_rows")

        zbytes = []
        w3_raw = []
        for b in range(B):
            w3_tile = loads.tile([P, G, PACK, O], BF16, name="w3_tile", bufs=B)
            w3_raw.append(w3_tile)
            for hf in range(HALVES):
                zb = loads.tile([P, SUB, R], U8, name="zb", bufs=STEPS, align_bytes=64)
                zbytes.append(zb)

        def load_z(s, n=SUB):
            b, hf = divmod(s, HALVES)
            for i in range(0, SUB, n):
                row = hf * ROWS + i * P
                nc.sync.dma_start(
                    out=zbytes[s][:, i : i + n, :],
                    in_=z2_bytes[row : row + n * P, b, :].rearrange("(i p) k -> p i k", p=P),
                )

        def load_w3(b):
            nc.sync.dma_start(
                out=w3_raw[b][:], in_=w3[b].rearrange("(g p j) o -> p g j o", p=P, j=PACK)
            )

        nc.vector.memset(warm[:], 0.0)
        nc.vector.memset(b2_rows[:], 0.0)
        nc.vector.memset(w1s_raw[:].bitcast(I32), 0)
        make_identity(nc, ident_f[:])
        make_identity(nc, ident_b[:])
        load_z(0, 2)
        nc.scalar.dma_start(
            out=kscale[:], in_=z2_scale.rearrange("a c (p t) -> p (a c t)", t=PACK)
        )
        nc.scalar.dma_start(
            out=b2_rows[0 : B * G, :], in_=b2.rearrange("b (g n) -> (b g) n", g=G)
        )
        nc.scalar.activation(out=warm[:], in_=warm[:], func=ACT.Relu)
        w1_words = sw1_words[0].rearrange("p n t -> p (n t)").bitcast(I32)
        for g in range(G):
            cols = slice(g * H // G, (g + 1) * H // G)
            nc.sync.dma_start(out=w1_raw[:, g, :], in_=w1_words[:, cols])
        for q in range(4):
            nc.sync.dma_start(
                out=w1s_raw[32 * q : 32 * q + 4, :].bitcast(I32),
                in_=sw1_scales[0, 4 * q : 4 * q + 4, :].bitcast(I32),
            )
        load_z(1)
        load_w3(0)
        load_z(2)
        load_z(3)
        load_z(4)
        load_w3(1)
        load_z(5)
        nc.sync.dma_start(
            out=b3_rows[:].rearrange("p b o -> p (b o)"),
            in_=b3.rearrange("b o -> (b o)").partition_broadcast(P),
        )
        for b in range(2, B):
            load_w3(b)
            for s in range(2 * b + 2, min(2 * b + 4, STEPS)):
                load_z(s)

        zs, zi, zt, zc, zsc = {}, {}, {}, {}, {}
        hp, hi, hc, hsc, acc1 = {}, {}, {}, {}, {}
        mixed, acc2, w3i, w3c, w3s = {}, {}, {}, {}, {}

        def permute_w1(g):
            nc.vector.tensor_copy(
                out=w1_codes[:, g], in_=w1_raw[:, g].rearrange("p (m t) -> p t m", t=PACK)
            )
            nc.vector.tensor_copy(
                out=w1_scales[:, g],
                in_=w1s_raw[:, g * H // G : (g + 1) * H // G].rearrange("p (m t) -> p t m", t=PACK),
            )

        def widen_z(s, copies):
            t = work.tile([P, SUB, R], BF16, name="zwide", bufs=2)
            zs[s] = t
            for i, copy in enumerate(copies):
                copy(out=t[:, i, :], in_=zbytes[s][:, i, :].bitcast(FP8))

        def transpose_z(s, halves):
            words = zs[s][:].rearrange("p i k -> p (i k)").bitcast(F32)
            zt.setdefault(s, [])
            for half in halves:
                bank = psum.tile([P, 2, 2, P], F32, name="zbank", bufs=2)
                zt[s].append(bank)
                for i in range(2):
                    base = 256 * (2 * half + i)
                    for u in range(2):
                        nc.tensor.transpose(
                            bank[:, u, i, :], words[:, base + u : base + 256 : 2], ident_f[:]
                        )

        def scale_z(s, half):
            if half == 0:
                t = work.tile([P, ROWS, PACK], BF16, name="zinter", bufs=2, align_bytes=64)
                zi[s] = t
            n = ROWS // 2
            nc.vector.tensor_tensor(
                out=zi[s][:, half * n : (half + 1) * n, :].rearrange("p n (u e) -> p n u e", e=2),
                in0=zt[s][half][:]
                .rearrange("p u i r -> p (u i r)")
                .bitcast(BF16)
                .rearrange("p (u n e) -> p n u e", u=2, e=2),
                in1=kscale[:]
                .rearrange("p (u e) -> p u e", e=2)
                .unsqueeze(1)
                .to_broadcast([P, n, 2, 2]),
                op=ALU.mult,
            )

        def quantize_z(s, cols):
            if cols.start == 0:
                c = work.tile([P, ROWS], U32, name="zcodes", bufs=2, align_bytes=64)
                e = work.tile([P, ROWS], U8, name="zexp", bufs=2, align_bytes=64)
                zc[s], zsc[s] = c, e
            nc.vector.quantize_mx(
                out=zc[s][:, cols].bitcast(FP8X4),
                scales=zsc[s][:, cols],
                in_=zi[s][:, cols, :].rearrange("p n j -> p (n j)"),
            )

        def hidden(s, g, cols, slots):
            for t in slots:
                if cols.start == 0:
                    bank = psum.tile([P, ROWS], F32, name="hbank", bufs=4)
                    acc1[s, g, t] = bank
                nc.tensor.matmul_mx(
                    out=acc1[s, g, t][:, cols],
                    lhsT=w1_codes[:, g, t, :].bitcast(FP8X4),
                    lhsT_scale=w1_scales[:, g, t, :],
                    rhs=zc[s][:, cols].bitcast(FP8X4),
                    rhs_scale=zsc[s][:, cols],
                    start=True,
                    stop=True,
                )

        def relu(s, g, cols):
            if g == 0 and cols.start == 0:
                planar = work.tile([P, G, PACK, ROWS], BF16, name="hplanar", bufs=3)
                inter = work.tile([P, G, ROWS, PACK], BF16, name="hinter", bufs=4, align_bytes=64)
                hp[s], hi[s] = planar, inter
            b = s // HALVES
            for t in range(PACK):
                nc.scalar.activation(
                    out=hp[s][:, g, t, cols],
                    in_=acc1[s, g, t][:, cols],
                    func=ACT.Relu,
                    bias=b2_cols[:, b * G + g, t : t + 1],
                )

        def interleave_vector(s, passes, cols):
            nc.vector.tensor_copy(
                out=hi[s][:, passes, cols, :].rearrange("p g (c i) t -> p g c t i", i=4),
                in_=hp[s][:, passes, :, cols].rearrange("p g t (c i) -> p g c t i", i=4),
            )

        def interleave_tensor(s, g):
            bank = psum.tile([P, NT, PACK], BF16, name="ibank", bufs=1)
            mixed[s, g] = bank
            for n in range(0, NT, NT // 2):
                nc.tensor.matmul(
                    bank[:, n : n + NT // 2, :],
                    lhsT=ident_b[:],
                    rhs=hp[s][:, g, :, n : n + NT // 2].rearrange("p t n -> p n t"),
                    start=True,
                    stop=True,
                )

        def copy_h(s, g):
            nc.scalar.copy(out=hi[s][:, g, 0:NT, :], in_=mixed[s, g][:])

        def quantize_h_part(s, g, cols):
            nc.vector.quantize_mx(
                out=hc[s][:, g, cols].bitcast(FP8X4),
                scales=hsc[s][:, g, cols],
                in_=hi[s][:, g, cols, :].rearrange("p n j -> p (n j)"),
            )

        def new_hidden_codes(s):
            c = work.tile([P, G, ROWS], U32, name="hcodes", bufs=2, align_bytes=64)
            e = work.tile([P, G, ROWS], U8, name="hexp", bufs=2, align_bytes=64)
            hc[s], hsc[s] = c, e

        def quantize_h(s):
            new_hidden_codes(s)
            c, e = hc[s], hsc[s]
            nc.vector.quantize_mx(
                out=c[:].rearrange("p g n -> p (g n)").bitcast(FP8X4),
                scales=e[:].rearrange("p g n -> p (g n)"),
                in_=hi[s][:].rearrange("p g n j -> p (g n j)"),
            )

        def interleave_w3(b):
            t = work.tile([P, G, O, PACK], BF16, name="w3inter", bufs=2, align_bytes=64)
            w3i[b] = t
            copy = nc.scalar.copy if b % 2 == 0 else nc.vector.tensor_copy
            copy(
                out=t[:].rearrange("p g (c i) t -> p g c t i", i=4),
                in_=w3_raw[b][:].rearrange("p g t (c i) -> p g c t i", i=4),
            )

        def quantize_w3(b):
            c = work.tile([P, G, O], U32, name="w3codes", bufs=B, align_bytes=64)
            e = work.tile([P, G, O], U8, name="w3exp", bufs=B, align_bytes=64)
            w3c[b], w3s[b] = c, e
            nc.vector.quantize_mx(
                out=c[:].rearrange("p g o -> p (g o)").bitcast(FP8X4),
                scales=e[:].rearrange("p g o -> p (g o)"),
                in_=w3i[b][:].rearrange("p g o j -> p (g o j)"),
            )

        def output(s, tiles):
            b = s // HALVES
            if tiles.start == 0:
                bank = psum.tile([P, SUB, O], F32, name="obank", bufs=1)
                acc2[s] = bank
            bank = acc2[s]
            for i in tiles:
                rows = slice(i * P, (i + 1) * P)
                for g in range(G):
                    nc.tensor.matmul_mx(
                        out=bank[:, i, :],
                        lhsT=hc[s][:, g, rows].bitcast(FP8X4),
                        lhsT_scale=hsc[s][:, g, rows],
                        rhs=w3c[b][:, g, :].bitcast(FP8X4),
                        rhs_scale=w3s[b][:, g, :],
                        start=(g == 0),
                        stop=(g == G - 1),
                    )

        def store(s, tiles):
            b, hf = divmod(s, HALVES)
            n = len(tiles)
            t = work.tile([P, SUB, O], F32, name="result", bufs=3)
            nc.vector.tensor_tensor(
                out=t[:, 0:n, :],
                in0=acc2[s][:, tiles.start : tiles.stop, :],
                in1=b3_rows[:, b, :].unsqueeze(1).to_broadcast([P, n, O]),
                op=ALU.add,
            )
            row = hf * ROWS + tiles.start * P
            nc.sync.dma_start(
                out=out[row : row + n * P, b, :].rearrange("(i p) o -> p i o", p=P),
                in_=t[:, 0:n, :],
            )

        whole, left, right = slice(0, ROWS), slice(0, ROWS // 2), slice(ROWS // 2, ROWS)
        both, rest = slice(0, G), slice(NT, ROWS)
        on_v, on_s, on_g = nc.vector.tensor_copy, nc.scalar.copy, nc.gpsimd.tensor_copy
        widen_z(0, [on_v, on_s, on_v, on_s])
        widen_z(1, [on_s, on_s, on_s, on_s])
        interleave_w3(0)
        transpose_z(0, [0, 1])
        bank = psum.tile([P, SUB, O], F32, name="obank", bufs=1)
        b2_words = b2_rows[:].bitcast(F32)
        for u in range(2):
            nc.tensor.transpose(bank[:, u, :], b2_words[:, u::2], ident_f[:])
        nc.scalar.copy(
            out=b2_cols[:].rearrange("p c t -> p (c t)").bitcast(F32).rearrange("p (c u) -> p c u", u=2),
            in_=bank[:, 0:2, 0 : B * G].rearrange("p u c -> p c u"),
        )
        scale_z(0, 0)
        permute_w1(0)
        quantize_z(0, left)
        transpose_z(1, [0])
        hidden(0, 0, left, range(PACK))
        relu(0, 0, left)
        scale_z(0, 1)
        transpose_z(1, [1])
        scale_z(1, 0)
        quantize_z(0, right)
        permute_w1(1)
        scale_z(1, 1)
        hidden(0, 0, right, range(PACK))
        relu(0, 0, right)
        widen_z(2, [on_g] * SUB)
        widen_z(3, [on_g] * SUB)

        last = STEPS - 1
        for s in range(STEPS):
            if s >= 1:
                hidden(s, 0, whole, range(PACK))
                relu(s, 0, whole)
                interleave_vector(s - 1, both, rest)
                interleave_tensor(s - 1, 1)
                copy_h(s - 1, 1)
            if s + 1 < STEPS:
                quantize_z(s + 1, whole)
            if s >= 2:
                quantize_h(s - 2)
            hidden(s, 1, whole, (0, 1))
            if s % HALVES == 0:
                quantize_w3(s // HALVES)
            if s + 2 < STEPS:
                transpose_z(s + 2, [0, 1])
                scale_z(s + 2, 0)
                scale_z(s + 2, 1)
            if s + 4 < STEPS:
                widen_z(s + 4, [on_g] * SUB)
            if s % HALVES == 1 and s // HALVES + 1 < B:
                interleave_w3(s // HALVES + 1)
            hidden(s, 1, whole, (2, 3))
            if s < last:
                relu(s, 1, whole)
                if s >= 2:
                    output(s - 2, range(SUB))
                    store(s - 2, range(SUB))
                interleave_tensor(s, 0)
                copy_h(s, 0)

        relu(last, 1, left)
        interleave_vector(last, slice(0, 1), rest)
        output(last - 2, range(SUB))
        interleave_tensor(last, 0)
        copy_h(last, 0)
        relu(last, 1, right)
        store(last - 2, range(SUB))
        quantize_h(last - 1)
        interleave_vector(last, slice(1, 2), left)
        output(last - 1, range(SUB))
        new_hidden_codes(last)
        quantize_h_part(last, 0, whole)
        interleave_vector(last, slice(1, 2), right)
        store(last - 1, range(SUB))
        for cols, tiles in ((left, range(0, 2)), (right, range(2, 4))):
            quantize_h_part(last, 1, cols)
            output(last, tiles)
        for tiles in (range(0, 2), range(2, 4)):
            store(last, tiles)
